import numpy as np
import ml_dtypes


def mxq(x, axis, fmt="e4m3"):
    dtype, down = {"e4m3": (ml_dtypes.float8_e4m3fn, 7), "e5m2": (ml_dtypes.float8_e5m2, 14)}[fmt]
    v = np.moveaxis(np.asarray(x, np.float32).astype(ml_dtypes.bfloat16).astype(np.float64), axis, -1)
    blocks = v.reshape(v.shape[:-1] + (-1, 32))
    amax = np.abs(blocks).max(-1, keepdims=True)
    byte = np.maximum(np.where(amax > 0, np.frexp(amax)[1] - 1 + 127, 0) - down, 1)
    scale = np.exp2(byte - 127.0)
    codes = (blocks / scale).astype(np.float32).astype(dtype).astype(np.float64)
    return np.moveaxis((codes * scale).reshape(v.shape), -1, axis)


WIDE = False


def mx_kscale(k):
    if not WIDE:
        return np.ones(k)
    levels = np.array([10, -10, 5, -5, 0])
    if k % 512:
        return np.exp2(np.random.permutation(np.resize(levels, k // 32))).repeat(32)
    a = np.empty((k // 512, 16))
    for p in range(k // 512):
        a[p, :8] = np.random.permutation(np.resize(levels, 8))
        for g in range(8):
            far = levels[np.abs(levels - a[p, g]) >= 10]
            a[p, g + 8] = far[np.random.randint(len(far))]
    return np.exp2(a.ravel()).repeat(32)


BF16 = ml_dtypes.bfloat16


def bf(x):
    return np.asarray(x, np.float32).astype(BF16)


def f64(x):
    return np.asarray(x).astype(np.float64)


B, K, N = 1024, 1024, 1024


def setup_inputs():
    s = mx_kscale(K)
    s = s / s.max()
    return {"x": bf(np.random.standard_normal((B, K)) * s),
            "W": bf(np.random.standard_normal((K, N)) * 0.4 / np.sqrt(K) / s[:, None]),
            "P": bf(np.random.standard_normal(N) * 0.3),
            "w": bf(0.8 + 0.1 * np.random.standard_normal(1)),
            "p": bf(0.5 + 0.1 * np.random.standard_normal(1)),
            "sine_w": bf(1.2 + 0.1 * np.random.standard_normal(1)),
            "cosine_w": bf(-0.7 + 0.1 * np.random.standard_normal(1))}


def core(x, W, P, w, p, sine_w, cosine_w):
    x = f64(x)
    original = f64(w) * x + f64(p)
    z = (mxq(x, 1, "e4m3") @ mxq(f64(W), 0, "e4m3")) + f64(P)
    periodic = f64(sine_w) * np.sin(z) + f64(cosine_w) * np.cos(z)
    return np.concatenate((original, periodic), axis=-1)


def e4m3fn_bytes(y):
    return np.clip(np.asarray(y, np.float64), -448.0, 448.0).astype(np.float32).astype(ml_dtypes.float8_e4m3fn).view(np.uint8)


def reference(x, W, P, w, p, sine_w, cosine_w):
    out = core(x, W, P, w, p, sine_w, cosine_w)
    s = np.max(np.abs(out), axis=-1, keepdims=True) / 448.0
    return out, e4m3fn_bytes(out / s)

@@ -1,0 +1,340 @@
+import math
+from contextlib import ExitStack
+
+import concourse.mybir as mybir
+from concourse.masks import make_identity
+
+FLOPS = 2 * 1024 * 1024 * 1024
+
+F32 = mybir.dt.float32
+BF16 = mybir.dt.bfloat16
+I32 = mybir.dt.int32
+U32 = mybir.dt.uint32
+U8 = mybir.dt.uint8
+FP8 = mybir.dt.float8_e4m3fn
+FP8X4 = mybir.dt.float8_e4m3fn_x4
+ALU = mybir.AluOpType
+ACT = mybir.ActivationFunctionType
+AX = mybir.AxisListType
+
+P = 128
+B, K, N = 1024, 1024, 1024
+NT = B // P
+NG = K // 512
+NH = N // 512
+H = 512
+INV2PI = 1.0 / (2.0 * math.pi)
+TWOPI = 2.0 * math.pi
+PI_SAFE = 3.1415925
+START_A = 1.542
+START_B = 0.618
+W_VEC_COLS = 336
+CAST_VEC_COLS = (0, 0, 0, 0, 0, 0, 512, 1344)
+
+
+def tile_time2vec_kernel(tc, x, W, Pb, w, p, sine_w, cosine_w, out_0, out_1):
+    nc = tc.nc
+    with ExitStack() as ctx:
+        const = ctx.enter_context(tc.tile_pool(name="const", bufs=1))
+        xgp = ctx.enter_context(tc.tile_pool(name="xgp", bufs=3))
+        ep = ctx.enter_context(tc.tile_pool(name="ep", bufs=3))
+        op = ctx.enter_context(tc.tile_pool(name="op", bufs=8))
+        o8p = ctx.enter_context(tc.tile_pool(name="o8p", bufs=3))
+        accp = ctx.enter_context(tc.psum_pool(name="accp", bufs=6))
+        xtp = ctx.enter_context(tc.psum_pool(name="xtp", bufs=2))
+
+        xs = {}
+        wraw = {}
+
+        def load_x(i):
+            t = const.tile([P, K], BF16, name="x%d" % i)
+            nc.sync.dma_start(out=t[:], in_=x[i * P:(i + 1) * P, :])
+            xs[i] = t
+
+        def load_w(g, h):
+            t = const.tile([P, 4, H], BF16, name="wraw%d%d" % (g, h))
+            nc.sync.dma_start(
+                out=t[:],
+                in_=W[g * 512:(g + 1) * 512, h * H:(h + 1) * H].rearrange("(p j) n -> p j n", j=4),
+            )
+            wraw[(g, h)] = t
+
+        scb = const.tile([P, 64], BF16, name="scb")
+        for j, sc_in in enumerate((w, p, sine_w, cosine_w)):
+            nc.sync.dma_start(out=scb[:, 16 * j:16 * j + 1], in_=sc_in.partition_broadcast(P))
+        zp = const.tile([P, N], BF16, name="zp")
+        nc.vector.memset(zp[:], 0.0)
+        ones = const.tile([P, P], BF16, name="ones")
+        nc.vector.memset(ones[:], 1.0)
+        load_w(0, 0)
+        load_w(1, 0)
+        nc.sync.dma_start(out=zp[0:1, :], in_=Pb.rearrange("(o n) -> o n", o=1))
+        load_x(0)
+        load_w(0, 1)
+        load_w(1, 1)
+        for i in range(1, NT):
+            load_x(i)
+
+        zero = const.tile([P, 1], F32, name="zero")
+        nc.gpsimd.memset(zero[:], 0.0)
+        mhalf = const.tile([P, 1], F32, name="mhalf")
+        nc.gpsimd.memset(mhalf[:], -0.5)
+        ident = const.tile([P, P], F32, name="ident")
+        make_identity(nc, ident[:])
+        warm = const.tile([P, 1], F32, name="warm")
+        nc.scalar.activation(out=warm[:], in_=zero[:], func=ACT.Sin)
+
+        wcodes = const.tile([P, NG, N], U32, name="wcodes", align_bytes=64)
+        wscales = const.tile([P, NG, N], U8, name="wscales", align_bytes=64)
+        wgrp = {}
+        for g in range(NG):
+            for h in range(NH):
+                wgrp[(g, h)] = const.tile([P, H, 4], BF16, name="wgrp%d%d" % (g, h), align_bytes=64)
+        pq = const.tile([P, N], F32, name="pq")
+        sc = const.tile([P, 4], F32, name="sc")
+        w_t, p_t, sw, cw = sc[:, 0:1], sc[:, 1:2], sc[:, 2:3], sc[:, 3:4]
+
+        ctx.enter_context(tc.manual_schedule())
+
+        pbs = []
+        for h in range(NH):
+            pb = accp.tile([P, H], F32, name="pb%d" % h, tag="acc")
+            nc.tensor.matmul(pb[:], lhsT=ones[:], rhs=zp[:, h * H:(h + 1) * H], start=True, stop=True)
+            pbs.append(pb)
+        nc.gpsimd.tensor_copy(out=sc[:], in_=scb[:, 0:64:16])
+
+        def small(name, cols=1):
+            return const.tile([P, cols], F32, name=name)
+
+        def gts(out, in0, s1, s2, op0, op1=None):
+            if op1 is None:
+                nc.gpsimd.tensor_scalar(out=out, in0=in0, scalar1=s1, scalar2=None, op0=op0)
+            else:
+                nc.gpsimd.tensor_scalar(out=out, in0=in0, scalar1=s1, scalar2=s2, op0=op0, op1=op1)
+
+        cw2 = small("cw2")
+        gts(cw2[:], cw, cw, 1e-30, ALU.mult, ALU.max)
+        q = small("q")
+        gts(q[:], sw, sw, cw2[:, 0:1], ALU.mult, ALU.add)
+        rn = small("rn")
+        nc.gpsimd.tensor_tensor(out=rn[:], in0=q[:], in1=mhalf[:], op=ALU.pow)
+        sh = small("sh")
+        gts(sh[:], sw, 0.0, 0.5, ALU.is_ge, ALU.subtract)
+        gs = small("gs")
+        gts(gs[:], rn[:], 2.0, sh[:, 0:1], ALU.mult, ALU.mult)
+        cs = small("cs", 2)
+        gts(cs[:], sc[:, 2:4], gs[:, 0:1], None, ALU.mult)
+        c0, s0 = cs[:, 0:1], cs[:, 1:2]
+        slope = small("slope")
+        gts(slope[:], c0, -START_B, START_A, ALU.mult, ALU.add)
+        angs = [small("ang%d" % it, 2) for it in range(3)]
+        sns = [small("sn%d" % it, 2) for it in range(3)]
+        gts(angs[0][:, 1:2], slope[:], s0, None, ALU.mult)
+        nc0 = small("nc0")
+        phs = small("phs")
+        amp = small("amp")
+
+        def quarter(it):
+            gts(angs[it][:, 0:1], angs[it][:, 1:2], 0.5 * math.pi, PI_SAFE, ALU.add, ALU.min)
+
+        def cos_sin(it):
+            nc.scalar.activation(out=sns[it][:], in_=angs[it][:], func=ACT.Sin)
+
+        def refine(it):
+            t1 = small("t1_%d" % it)
+            gts(t1[:], sns[it][:, 0:1], s0, angs[it][:, 1:2], ALU.mult, ALU.add)
+            gts(angs[it + 1][:, 1:2], sns[it][:, 1:2], nc0[:, 0:1], t1[:, 0:1], ALU.mult, ALU.add)
+
+        quarter(0)
+        gts(nc0[:], c0, -1.0, None, ALU.mult)
+        phi = angs[2][:, 1:2]
+
+        def w_copy_vec(g, h):
+            cv = W_VEC_COLS
+            nc.vector.tensor_copy(out=wgrp[(g, h)][:, 0:cv, :], in_=wraw[(g, h)][:, :, 0:cv].rearrange("p j n -> p n j"))
+
+        def w_copy_act(g, h):
+            cv = W_VEC_COLS
+            nc.scalar.copy(out=wgrp[(g, h)][:, cv:H, :], in_=wraw[(g, h)][:, :, cv:H].rearrange("p j n -> p n j"))
+
+        def w_quant(g, h):
+            nc.vector.quantize_mx(
+                out=wcodes[:, g, h * H:(h + 1) * H].bitcast(FP8X4),
+                scales=wscales[:, g, h * H:(h + 1) * H],
+                in_=wgrp[(g, h)][:].rearrange("p n j -> p (n j)"),
+            )
+
+        xt, xg, xc, xsc, acc, v, n, fr, s, o, st = {}, {}, {}, {}, {}, {}, {}, {}, {}, {}, {}
+
+        def x_transpose(i):
+            words = xs[i][:].bitcast(F32)
+            xt[i] = xtp.tile([P, NG, 2, P], F32, name="xt", tag="xt")
+            for g in range(NG):
+                for u in range(2):
+                    nc.tensor.transpose(xt[i][:, g, u, :], words[:, 256 * g + u:256 * (g + 1):2], ident[:])
+
+        def x_copy(i):
+            xg[i] = xgp.tile([P, 4 * NG * P], BF16, name="xg", tag="xg", align_bytes=64)
+            nc.scalar.copy(
+                out=xg[i][:].bitcast(F32).rearrange("p (g r u) -> p g r u", g=NG, u=2),
+                in_=xt[i][:].rearrange("p g u r -> p g r u"),
+            )
+
+        def x_quant(i):
+            xc[i] = xgp.tile([P, NG * P], U32, name="xc", tag="xc", align_bytes=64)
+            xsc[i] = xgp.tile([P, NG * P], U8, name="xsc", tag="xsc", align_bytes=64)
+            nc.vector.quantize_mx(out=xc[i][:].bitcast(FP8X4), scales=xsc[i][:], in_=xg[i][:])
+
+        def mm(i, halves=(0, 1)):
+            for h in halves:
+                acc[(i, h)] = accp.tile([P, H], F32, name="acc", tag="acc")
+                for g in range(NG):
+                    nc.tensor.matmul_mx(
+                        out=acc[(i, h)][:],
+                        lhsT=xc[i][:, g * P:(g + 1) * P].bitcast(FP8X4),
+                        lhsT_scale=xsc[i][:, g * P:(g + 1) * P],
+                        rhs=wcodes[:, g, h * H:(h + 1) * H].bitcast(FP8X4),
+                        rhs_scale=wscales[:, g, h * H:(h + 1) * H],
+                        start=(g == 0),
+                        stop=(g == NG - 1),
+                    )
+
+        def turns(i, h):
+            if h == 0:
+                v[i] = ep.tile([P, N], F32, name="v", tag="v")
+                n[i] = ep.tile([P, N], I32, name="n", tag="n")
+            cols = slice(h * H, (h + 1) * H)
+            nc.vector.scalar_tensor_tensor(out=v[i][:, cols], in0=acc[(i, h)][:], scalar=INV2PI, in1=pq[:, cols],
+                                           op0=ALU.mult, op1=ALU.add)
+            nc.gpsimd.tensor_scalar(out=n[i][:, cols], in0=v[i][:, cols], scalar1=1.0, scalar2=phs[:, 0:1],
+                                    op0=ALU.mult, op1=ALU.add)
+
+        def frac(i):
+            fr[i] = ep.tile([P, N], F32, name="fr", tag="fr")
+            nc.vector.tensor_tensor(out=fr[i][:], in0=v[i][:], in1=n[i][:], op=ALU.subtract)
+
+        def sine(i):
+            s[i] = ep.tile([P, N], F32, name="s", tag="s")
+            nc.scalar.activation(out=s[i][:], in_=fr[i][:], func=ACT.Sin, bias=phi, scale=TWOPI)
+
+        def periodic(i):
+            if i == NT - 1:
+                nc.vector.tensor_scalar(out=o[i][:, N:2 * N], in0=s[i][:], scalar1=amp[:, 0:1], scalar2=None,
+                                        op0=ALU.mult)
+            else:
+                nc.scalar.activation(out=o[i][:, N:2 * N], in_=s[i][:], func=ACT.Identity, scale=amp[:, 0:1])
+            nc.sync.dma_start(out=out_0[i * P:(i + 1) * P, N:2 * N], in_=o[i][:, N:2 * N])
+
+        def linear(i):
+            o[i] = op.tile([P, 2 * N], F32, name="o", tag="o")
+            for h in range(2):
+                cols = slice(h * H, (h + 1) * H)
+                nc.gpsimd.tensor_scalar(out=o[i][:, cols], in0=xs[i][:, cols], scalar1=w_t, scalar2=p_t,
+                                        op0=ALU.mult, op1=ALU.add)
+            nc.sync.dma_start(out=out_0[i * P:(i + 1) * P, 0:N], in_=o[i][:, 0:N])
+
+        def amax_linear(i):
+            st[i] = op.tile([P, 4], F32, name="st", tag="st")
+            nc.vector.tensor_reduce(out=st[i][:, 0:1], in_=o[i][:, 0:N], axis=AX.X, op=ALU.max,
+                                    apply_absolute_value=True)
+
+        def amax_periodic(i):
+            nc.vector.tensor_reduce(out=st[i][:, 1:2], in_=o[i][:, N:2 * N], axis=AX.X, op=ALU.max,
+                                    apply_absolute_value=True)
+
+        def q_scale(i):
+            nc.vector.tensor_scalar(out=st[i][:, 2:3], in0=st[i][:, 1:2], scalar1=st[i][:, 0:1], scalar2=1.0 / 448.0,
+                                    op0=ALU.max, op1=ALU.mult)
+
+        def r_scale(i):
+            nc.vector.reciprocal(out=st[i][:, 3:4], in_=st[i][:, 2:3])
+
+        o8 = {}
+
+        def cast_vec(i):
+            o8[i] = o8p.tile([P, 2 * N], FP8, name="o8", tag="o8")
+            cc = 2 * N - CAST_VEC_COLS[i]
+            if cc < 2 * N:
+                nc.vector.tensor_scalar(out=o8[i][:, cc:2 * N], in0=o[i][:, cc:2 * N], scalar1=st[i][:, 3:4],
+                                        scalar2=None, op0=ALU.mult, saturate=False)
+
+        def cast_act(i):
+            cc = 2 * N - CAST_VEC_COLS[i]
+            nc.scalar.activation(out=o8[i][:, 0:cc], in_=o[i][:, 0:cc], func=ACT.Identity, bias=zero[:, 0:1],
+                                 scale=st[i][:, 3:4], saturate=False)
+            nc.sync.dma_start(out=out_1[i * P:(i + 1) * P, :], in_=o8[i][:].bitcast(U8))
+
+        w_copy_vec(0, 0)
+        w_copy_act(0, 0)
+        w_copy_vec(1, 0)
+        w_copy_act(1, 0)
+        w_quant(0, 0)
+        w_quant(1, 0)
+        w_copy_vec(0, 1)
+        w_copy_act(0, 1)
+        x_transpose(0)
+        x_copy(0)
+        x_quant(0)
+        mm(0, (0,))
+        w_copy_vec(1, 1)
+        w_copy_act(1, 1)
+        w_quant(0, 1)
+        w_quant(1, 1)
+        cos_sin(0)
+        refine(0)
+        quarter(1)
+        for h in range(NH):
+            nc.scalar.activation(out=pq[:, h * H:(h + 1) * H], in_=pbs[h][:], func=ACT.Copy, scale=INV2PI)
+        cos_sin(1)
+        refine(1)
+        gts(phs[:], phi, INV2PI, None, ALU.mult)
+        quarter(2)
+        turns(0, 0)
+        x_transpose(1)
+        x_transpose(2)
+        mm(0, (1,))
+        x_copy(1)
+        x_quant(1)
+        turns(0, 1)
+        x_transpose(3)
+        x_copy(2)
+        x_quant(2)
+        mm(1)
+        x_transpose(4)
+        cos_sin(2)
+        u1 = small("u1")
+        gts(u1[:], sns[2][:, 1:2], cw, None, ALU.mult)
+        gts(amp[:], sns[2][:, 0:1], sw, u1[:, 0:1], ALU.mult, ALU.add)
+        x_copy(3)
+        x_transpose(5)
+
+        for k in range(NT + 2):
+            if 1 <= k < NT:
+                turns(k, 0)
+                turns(k, 1)
+            if 1 <= k <= NT:
+                sine(k - 1)
+                amax_linear(k - 1)
+                periodic(k - 1)
+            if k < NT:
+                linear(k)
+            if 1 <= k <= NT:
+                amax_periodic(k - 1)
+            if k < NT:
+                frac(k)
+            if 1 <= k <= NT:
+                q_scale(k - 1)
+            if 3 <= k + 2 < NT:
+                x_quant(k + 2)
+            if k + 2 < NT:
+                mm(k + 2)
+            if k >= 2:
+                cast_vec(k - 2)
+            if 1 <= k <= NT:
+                r_scale(k - 1)
+            if k >= 1 and k + 3 < NT:
+                x_copy(k + 3)
+            if k >= 1 and k + 5 < NT:
+                x_transpose(k + 5)
+            if k >= 2:
+                cast_act(k - 2)

@@ -29,7 +29,7 @@ PI_SAFE = 3.1415925
 START_A = 1.542
 START_B = 0.618
 W_VEC_COLS = 336
-CAST_VEC_COLS = (0, 0, 0, 0, 0, 0, 512, 1344)
+CAST_VEC_COLS = (384, 384, 384, 384, 384, 384, 768, 1344)
 
 
 def tile_time2vec_kernel(tc, x, W, Pb, w, p, sine_w, cosine_w, out_0, out_1):
@@ -206,7 +206,9 @@ def tile_time2vec_kernel(tc, x, W, Pb, w, p, sine_w, cosine_w, out_0, out_1):
             cols = slice(h * H, (h + 1) * H)
             nc.vector.scalar_tensor_tensor(out=v[i][:, cols], in0=acc[(i, h)][:], scalar=INV2PI, in1=pq[:, cols],
                                            op0=ALU.mult, op1=ALU.add)
-            nc.gpsimd.tensor_scalar(out=n[i][:, cols], in0=v[i][:, cols], scalar1=1.0, scalar2=phs[:, 0:1],
+
+        def whole_turns(i):
+            nc.vector.tensor_scalar(out=n[i][:], in0=v[i][:], scalar1=1.0, scalar2=phs[:, 0:1],
                                     op0=ALU.mult, op1=ALU.add)
 
         def frac(i):
@@ -227,10 +229,7 @@ def tile_time2vec_kernel(tc, x, W, Pb, w, p, sine_w, cosine_w, out_0, out_1):
 
         def linear(i):
             o[i] = op.tile([P, 2 * N], F32, name="o", tag="o")
-            for h in range(2):
-                cols = slice(h * H, (h + 1) * H)
-                nc.gpsimd.tensor_scalar(out=o[i][:, cols], in0=xs[i][:, cols], scalar1=w_t, scalar2=p_t,
-                                        op0=ALU.mult, op1=ALU.add)
+            nc.scalar.activation(out=o[i][:, 0:N], in_=xs[i][:], func=ACT.Identity, bias=p_t, scale=w_t)
             nc.sync.dma_start(out=out_0[i * P:(i + 1) * P, 0:N], in_=o[i][:, 0:N])
 
         def amax_linear(i):
@@ -318,6 +317,7 @@ def tile_time2vec_kernel(tc, x, W, Pb, w, p, sine_w, cosine_w, out_0, out_1):
                 periodic(k - 1)
             if k < NT:
                 linear(k)
+                whole_turns(k)
             if 1 <= k <= NT:
                 amax_periodic(k - 1)
             if k < NT:

@@ -29,7 +29,7 @@ PI_SAFE = 3.1415925
 START_A = 1.542
 START_B = 0.618
 W_VEC_COLS = 336
-CAST_VEC_COLS = (384, 384, 384, 384, 384, 384, 768, 1344)
+CAST_VEC_COLS = (0, 0, 0, 0, 0, 640, 768, 1280)
 
 
 def tile_time2vec_kernel(tc, x, W, Pb, w, p, sine_w, cosine_w, out_0, out_1):
@@ -206,9 +206,7 @@ def tile_time2vec_kernel(tc, x, W, Pb, w, p, sine_w, cosine_w, out_0, out_1):
             cols = slice(h * H, (h + 1) * H)
             nc.vector.scalar_tensor_tensor(out=v[i][:, cols], in0=acc[(i, h)][:], scalar=INV2PI, in1=pq[:, cols],
                                            op0=ALU.mult, op1=ALU.add)
-
-        def whole_turns(i):
-            nc.vector.tensor_scalar(out=n[i][:], in0=v[i][:], scalar1=1.0, scalar2=phs[:, 0:1],
+            nc.gpsimd.tensor_scalar(out=n[i][:, cols], in0=v[i][:, cols], scalar1=1.0, scalar2=phs[:, 0:1],
                                     op0=ALU.mult, op1=ALU.add)
 
         def frac(i):
@@ -229,7 +227,10 @@ def tile_time2vec_kernel(tc, x, W, Pb, w, p, sine_w, cosine_w, out_0, out_1):
 
         def linear(i):
             o[i] = op.tile([P, 2 * N], F32, name="o", tag="o")
-            nc.scalar.activation(out=o[i][:, 0:N], in_=xs[i][:], func=ACT.Identity, bias=p_t, scale=w_t)
+            for h in range(2):
+                cols = slice(h * H, (h + 1) * H)
+                nc.gpsimd.tensor_scalar(out=o[i][:, cols], in0=xs[i][:, cols], scalar1=w_t, scalar2=p_t,
+                                        op0=ALU.mult, op1=ALU.add)
             nc.sync.dma_start(out=out_0[i * P:(i + 1) * P, 0:N], in_=o[i][:, 0:N])
 
         def amax_linear(i):
@@ -279,6 +280,7 @@ def tile_time2vec_kernel(tc, x, W, Pb, w, p, sine_w, cosine_w, out_0, out_1):
         w_copy_act(1, 1)
         w_quant(0, 1)
         w_quant(1, 1)
+        linear(0)
         cos_sin(0)
         refine(0)
         quarter(1)
@@ -307,34 +309,34 @@ def tile_time2vec_kernel(tc, x, W, Pb, w, p, sine_w, cosine_w, out_0, out_1):
         x_copy(3)
         x_transpose(5)
 
-        for k in range(NT + 2):
+        for k in range(NT + 3):
             if 1 <= k < NT:
                 turns(k, 0)
                 turns(k, 1)
             if 1 <= k <= NT:
                 sine(k - 1)
-                amax_linear(k - 1)
+            if 2 <= k <= NT + 1:
+                amax_periodic(k - 2)
+            if 1 <= k <= NT:
                 periodic(k - 1)
+            if k + 1 < NT:
+                linear(k + 1)
             if k < NT:
-                linear(k)
-                whole_turns(k)
-            if 1 <= k <= NT:
-                amax_periodic(k - 1)
-            if k < NT:
+                amax_linear(k)
                 frac(k)
-            if 1 <= k <= NT:
-                q_scale(k - 1)
+            if 2 <= k <= NT + 1:
+                q_scale(k - 2)
             if 3 <= k + 2 < NT:
                 x_quant(k + 2)
             if k + 2 < NT:
                 mm(k + 2)
-            if k >= 2:
-                cast_vec(k - 2)
-            if 1 <= k <= NT:
-                r_scale(k - 1)
+            if k >= 3:
+                cast_vec(k - 3)
+            if 2 <= k <= NT + 1:
+                r_scale(k - 2)
             if k >= 1 and k + 3 < NT:
                 x_copy(k + 3)
             if k >= 1 and k + 5 < NT:
                 x_transpose(k + 5)
-            if k >= 2:
-                cast_act(k - 2)
+            if k >= 3:
+                cast_act(k - 3)

@@ -25,7 +25,6 @@ NH = N // 512
 H = 512
 INV2PI = 1.0 / (2.0 * math.pi)
 TWOPI = 2.0 * math.pi
-PI_SAFE = 3.1415925
 START_A = 1.542
 START_B = 0.618
 W_VEC_COLS = 336
@@ -66,10 +65,10 @@ def tile_time2vec_kernel(tc, x, W, Pb, w, p, sine_w, cosine_w, out_0, out_1):
         nc.vector.memset(zp[:], 0.0)
         ones = const.tile([P, P], BF16, name="ones")
         nc.vector.memset(ones[:], 1.0)
-        load_w(0, 0)
-        load_w(1, 0)
         nc.sync.dma_start(out=zp[0:1, :], in_=Pb.rearrange("(o n) -> o n", o=1))
         load_x(0)
+        load_w(0, 0)
+        load_w(1, 0)
         load_w(0, 1)
         load_w(1, 1)
         for i in range(1, NT):
@@ -101,7 +100,6 @@ def tile_time2vec_kernel(tc, x, W, Pb, w, p, sine_w, cosine_w, out_0, out_1):
             pb = accp.tile([P, H], F32, name="pb%d" % h, tag="acc")
             nc.tensor.matmul(pb[:], lhsT=ones[:], rhs=zp[:, h * H:(h + 1) * H], start=True, stop=True)
             pbs.append(pb)
-        nc.gpsimd.tensor_copy(out=sc[:], in_=scb[:, 0:64:16])
 
         def small(name, cols=1):
             return const.tile([P, cols], F32, name=name)
@@ -111,6 +109,12 @@ def tile_time2vec_kernel(tc, x, W, Pb, w, p, sine_w, cosine_w, out_0, out_1):
                 nc.gpsimd.tensor_scalar(out=out, in0=in0, scalar1=s1, scalar2=None, op0=op0)
             else:
                 nc.gpsimd.tensor_scalar(out=out, in0=in0, scalar1=s1, scalar2=s2, op0=op0, op1=op1)
+
+        halfpi = small("halfpi")
+        gts(halfpi[:], zero[:], 0.0, 0.5 * math.pi, ALU.mult, ALU.add)
+        start_a = small("start_a")
+        gts(start_a[:], zero[:], 0.0, START_A, ALU.mult, ALU.add)
+        nc.gpsimd.tensor_copy(out=sc[:], in_=scb[:, 0:64:16])
 
         cw2 = small("cw2")
         gts(cw2[:], cw, cw, 1e-30, ALU.mult, ALU.max)
@@ -123,31 +127,48 @@ def tile_time2vec_kernel(tc, x, W, Pb, w, p, sine_w, cosine_w, out_0, out_1):
         gs = small("gs")
         gts(gs[:], rn[:], 2.0, sh[:, 0:1], ALU.mult, ALU.mult)
         cs = small("cs", 2)
-        gts(cs[:], sc[:, 2:4], gs[:, 0:1], None, ALU.mult)
         c0, s0 = cs[:, 0:1], cs[:, 1:2]
         slope = small("slope")
-        gts(slope[:], c0, -START_B, START_A, ALU.mult, ALU.add)
-        angs = [small("ang%d" % it, 2) for it in range(3)]
-        sns = [small("sn%d" % it, 2) for it in range(3)]
-        gts(angs[0][:, 1:2], slope[:], s0, None, ALU.mult)
         nc0 = small("nc0")
+        angs = [small("ang%d" % it) for it in range(3)]
         phs = small("phs")
         amp = small("amp")
+        phi = angs[2][:, 0:1]
 
-        def quarter(it):
-            gts(angs[it][:, 0:1], angs[it][:, 1:2], 0.5 * math.pi, PI_SAFE, ALU.add, ALU.min)
+        def act(out, in_, func, scale=None, bias=None):
+            if scale is None and bias is None:
+                nc.scalar.activation(out=out, in_=in_, func=func)
+            elif bias is None:
+                nc.scalar.activation(out=out, in_=in_, func=func, scale=scale)
+            else:
+                nc.scalar.activation(out=out, in_=in_, func=func, scale=scale, bias=bias)
 
-        def cos_sin(it):
-            nc.scalar.activation(out=sns[it][:], in_=angs[it][:], func=ACT.Sin)
+        def first_angle():
+            act(cs[:], sc[:, 2:4], ACT.Identity, scale=gs[:, 0:1])
+            act(slope[:], c0, ACT.Identity, scale=-START_B, bias=start_a[:, 0:1])
+            act(nc0[:], c0, ACT.Copy, scale=-1.0)
+            act(angs[0][:], slope[:], ACT.Identity, scale=s0)
+
+        def sin_cos(it):
+            ab = small("ab%d" % it)
+            sn = small("sn%d" % it)
+            cn = small("cn%d" % it)
+            act(ab[:], angs[it][:], ACT.Abs)
+            act(sn[:], angs[it][:], ACT.Sin)
+            act(cn[:], ab[:], ACT.Sin, scale=-1.0, bias=halfpi[:, 0:1])
+            return sn, cn
 
         def refine(it):
+            sn, cn = sin_cos(it)
             t1 = small("t1_%d" % it)
-            gts(t1[:], sns[it][:, 0:1], s0, angs[it][:, 1:2], ALU.mult, ALU.add)
-            gts(angs[it + 1][:, 1:2], sns[it][:, 1:2], nc0[:, 0:1], t1[:, 0:1], ALU.mult, ALU.add)
+            act(t1[:], sn[:], ACT.Identity, scale=nc0[:, 0:1], bias=angs[it][:, 0:1])
+            act(angs[it + 1][:], cn[:], ACT.Identity, scale=s0, bias=t1[:, 0:1])
 
-        quarter(0)
-        gts(nc0[:], c0, -1.0, None, ALU.mult)
-        phi = angs[2][:, 1:2]
+        def amplitude():
+            sn, cn = sin_cos(2)
+            u1 = small("u1")
+            act(u1[:], sn[:], ACT.Identity, scale=cw)
+            act(amp[:], cn[:], ACT.Identity, scale=sw, bias=u1[:, 0:1])
 
         def w_copy_vec(g, h):
             cv = W_VEC_COLS
@@ -233,21 +254,17 @@ def tile_time2vec_kernel(tc, x, W, Pb, w, p, sine_w, cosine_w, out_0, out_1):
                                         op0=ALU.mult, op1=ALU.add)
             nc.sync.dma_start(out=out_0[i * P:(i + 1) * P, 0:N], in_=o[i][:, 0:N])
 
-        def amax_linear(i):
-            st[i] = op.tile([P, 4], F32, name="st", tag="st")
-            nc.vector.tensor_reduce(out=st[i][:, 0:1], in_=o[i][:, 0:N], axis=AX.X, op=ALU.max,
-                                    apply_absolute_value=True)
-
-        def amax_periodic(i):
-            nc.vector.tensor_reduce(out=st[i][:, 1:2], in_=o[i][:, N:2 * N], axis=AX.X, op=ALU.max,
+        def row_amax(i):
+            st[i] = op.tile([P, 24], F32, name="st", tag="st")
+            nc.vector.tensor_reduce(out=st[i][:, 0:1], in_=o[i][:], axis=AX.X, op=ALU.max,
                                     apply_absolute_value=True)
 
         def q_scale(i):
-            nc.vector.tensor_scalar(out=st[i][:, 2:3], in0=st[i][:, 1:2], scalar1=st[i][:, 0:1], scalar2=1.0 / 448.0,
-                                    op0=ALU.max, op1=ALU.mult)
+            nc.vector.tensor_scalar(out=st[i][:, 8:9], in0=st[i][:, 0:1], scalar1=1.0 / 448.0, scalar2=None,
+                                    op0=ALU.mult)
 
         def r_scale(i):
-            nc.vector.reciprocal(out=st[i][:, 3:4], in_=st[i][:, 2:3])
+            nc.vector.reciprocal(out=st[i][:, 16:17], in_=st[i][:, 8:9])
 
         o8 = {}
 
@@ -255,45 +272,42 @@ def tile_time2vec_kernel(tc, x, W, Pb, w, p, sine_w, cosine_w, out_0, out_1):
             o8[i] = o8p.tile([P, 2 * N], FP8, name="o8", tag="o8")
             cc = 2 * N - CAST_VEC_COLS[i]
             if cc < 2 * N:
-                nc.vector.tensor_scalar(out=o8[i][:, cc:2 * N], in0=o[i][:, cc:2 * N], scalar1=st[i][:, 3:4],
+                nc.vector.tensor_scalar(out=o8[i][:, cc:2 * N], in0=o[i][:, cc:2 * N], scalar1=st[i][:, 16:17],
                                         scalar2=None, op0=ALU.mult, saturate=False)
 
         def cast_act(i):
             cc = 2 * N - CAST_VEC_COLS[i]
             nc.scalar.activation(out=o8[i][:, 0:cc], in_=o[i][:, 0:cc], func=ACT.Identity, bias=zero[:, 0:1],
-                                 scale=st[i][:, 3:4], saturate=False)
+                                 scale=st[i][:, 16:17], saturate=False)
             nc.sync.dma_start(out=out_1[i * P:(i + 1) * P, :], in_=o8[i][:].bitcast(U8))
 
-        w_copy_vec(0, 0)
-        w_copy_act(0, 0)
-        w_copy_vec(1, 0)
-        w_copy_act(1, 0)
-        w_quant(0, 0)
-        w_quant(1, 0)
-        w_copy_vec(0, 1)
-        w_copy_act(0, 1)
+        for h in range(NH):
+            nc.scalar.activation(out=pq[:, h * H:(h + 1) * H], in_=pbs[h][:], func=ACT.Copy, scale=INV2PI)
         x_transpose(0)
         x_copy(0)
+        w_copy_vec(0, 0)
+        w_copy_act(0, 0)
         x_quant(0)
+        w_copy_vec(1, 0)
+        w_copy_act(1, 0)
+        first_angle()
+        refine(0)
+        w_quant(0, 0)
+        w_copy_vec(0, 1)
+        w_copy_act(0, 1)
+        w_quant(1, 0)
         mm(0, (0,))
         w_copy_vec(1, 1)
         w_copy_act(1, 1)
+        refine(1)
+        act(phs[:], phi, ACT.Copy, scale=INV2PI)
+        amplitude()
         w_quant(0, 1)
         w_quant(1, 1)
-        linear(0)
-        cos_sin(0)
-        refine(0)
-        quarter(1)
-        for h in range(NH):
-            nc.scalar.activation(out=pq[:, h * H:(h + 1) * H], in_=pbs[h][:], func=ACT.Copy, scale=INV2PI)
-        cos_sin(1)
-        refine(1)
-        gts(phs[:], phi, INV2PI, None, ALU.mult)
-        quarter(2)
-        turns(0, 0)
         x_transpose(1)
         x_transpose(2)
         mm(0, (1,))
+        turns(0, 0)
         x_copy(1)
         x_quant(1)
         turns(0, 1)
@@ -302,10 +316,6 @@ def tile_time2vec_kernel(tc, x, W, Pb, w, p, sine_w, cosine_w, out_0, out_1):
         x_quant(2)
         mm(1)
         x_transpose(4)
-        cos_sin(2)
-        u1 = small("u1")
-        gts(u1[:], sns[2][:, 1:2], cw, None, ALU.mult)
-        gts(amp[:], sns[2][:, 0:1], sw, u1[:, 0:1], ALU.mult, ALU.add)
         x_copy(3)
         x_transpose(5)
 
@@ -316,13 +326,11 @@ def tile_time2vec_kernel(tc, x, W, Pb, w, p, sine_w, cosine_w, out_0, out_1):
             if 1 <= k <= NT:
                 sine(k - 1)
             if 2 <= k <= NT + 1:
-                amax_periodic(k - 2)
+                row_amax(k - 2)
             if 1 <= k <= NT:
                 periodic(k - 1)
-            if k + 1 < NT:
-                linear(k + 1)
             if k < NT:
-                amax_linear(k)
+                linear(k)
                 frac(k)
             if 2 <= k <= NT + 1:
                 q_scale(k - 2)

@@ -65,10 +65,10 @@ def tile_time2vec_kernel(tc, x, W, Pb, w, p, sine_w, cosine_w, out_0, out_1):
         nc.vector.memset(zp[:], 0.0)
         ones = const.tile([P, P], BF16, name="ones")
         nc.vector.memset(ones[:], 1.0)
-        nc.sync.dma_start(out=zp[0:1, :], in_=Pb.rearrange("(o n) -> o n", o=1))
-        load_x(0)
         load_w(0, 0)
+        nc.sync.dma_start(out=zp[0:1, :], in_=Pb.rearrange("(o n) -> o n", o=1))
         load_w(1, 0)
+        load_x(0)
         load_w(0, 1)
         load_w(1, 1)
         for i in range(1, NT):
@@ -114,18 +114,19 @@ def tile_time2vec_kernel(tc, x, W, Pb, w, p, sine_w, cosine_w, out_0, out_1):
         gts(halfpi[:], zero[:], 0.0, 0.5 * math.pi, ALU.mult, ALU.add)
         start_a = small("start_a")
         gts(start_a[:], zero[:], 0.0, START_A, ALU.mult, ALU.add)
-        nc.gpsimd.tensor_copy(out=sc[:], in_=scb[:, 0:64:16])
 
-        cw2 = small("cw2")
-        gts(cw2[:], cw, cw, 1e-30, ALU.mult, ALU.max)
-        q = small("q")
-        gts(q[:], sw, sw, cw2[:, 0:1], ALU.mult, ALU.add)
-        rn = small("rn")
-        nc.gpsimd.tensor_tensor(out=rn[:], in0=q[:], in1=mhalf[:], op=ALU.pow)
-        sh = small("sh")
-        gts(sh[:], sw, 0.0, 0.5, ALU.is_ge, ALU.subtract)
-        gs = small("gs")
-        gts(gs[:], rn[:], 2.0, sh[:, 0:1], ALU.mult, ALU.mult)
+        nc.vector.tensor_copy(out=sc[:], in_=scb[:, 0:64:16])
+        sgh = small("sgh")
+        nc.vector.tensor_scalar(out=sgh[:], in0=sw, scalar1=0.0, scalar2=0.5, op0=ALU.is_ge, op1=ALU.subtract)
+        hv = small("hv", 2)
+        nc.vector.tensor_scalar(out=hv[:], in0=sc[:, 2:4], scalar1=sgh[:, 0:1], scalar2=None, op0=ALU.mult)
+        b2 = small("b2")
+        nc.vector.tensor_scalar(out=b2[:], in0=hv[:, 1:2], scalar1=hv[:, 1:2], scalar2=1e-30, op0=ALU.mult, op1=ALU.max)
+        q4 = small("q4")
+        nc.vector.tensor_scalar(out=q4[:], in0=hv[:, 0:1], scalar1=hv[:, 0:1], scalar2=b2[:, 0:1], op0=ALU.mult,
+                                op1=ALU.add)
+        rn2 = small("rn2")
+        nc.gpsimd.tensor_tensor(out=rn2[:], in0=q4[:], in1=mhalf[:], op=ALU.pow)
         cs = small("cs", 2)
         c0, s0 = cs[:, 0:1], cs[:, 1:2]
         slope = small("slope")
@@ -144,7 +145,7 @@ def tile_time2vec_kernel(tc, x, W, Pb, w, p, sine_w, cosine_w, out_0, out_1):
                 nc.scalar.activation(out=out, in_=in_, func=func, scale=scale, bias=bias)
 
         def first_angle():
-            act(cs[:], sc[:, 2:4], ACT.Identity, scale=gs[:, 0:1])
+            act(cs[:], hv[:], ACT.Identity, scale=rn2[:, 0:1])
             act(slope[:], c0, ACT.Identity, scale=-START_B, bias=start_a[:, 0:1])
             act(nc0[:], c0, ACT.Copy, scale=-1.0)
             act(angs[0][:], slope[:], ACT.Identity, scale=s0)
@@ -254,14 +255,18 @@ def tile_time2vec_kernel(tc, x, W, Pb, w, p, sine_w, cosine_w, out_0, out_1):
                                         op0=ALU.mult, op1=ALU.add)
             nc.sync.dma_start(out=out_0[i * P:(i + 1) * P, 0:N], in_=o[i][:, 0:N])
 
-        def row_amax(i):
+        def amax_linear(i):
             st[i] = op.tile([P, 24], F32, name="st", tag="st")
-            nc.vector.tensor_reduce(out=st[i][:, 0:1], in_=o[i][:], axis=AX.X, op=ALU.max,
+            nc.vector.tensor_reduce(out=st[i][:, 0:1], in_=o[i][:, 0:N], axis=AX.X, op=ALU.max,
+                                    apply_absolute_value=True)
+
+        def amax_periodic(i):
+            nc.vector.tensor_reduce(out=st[i][:, 1:2], in_=o[i][:, N:2 * N], axis=AX.X, op=ALU.max,
                                     apply_absolute_value=True)
 
         def q_scale(i):
-            nc.vector.tensor_scalar(out=st[i][:, 8:9], in0=st[i][:, 0:1], scalar1=1.0 / 448.0, scalar2=None,
-                                    op0=ALU.mult)
+            nc.vector.tensor_scalar(out=st[i][:, 8:9], in0=st[i][:, 1:2], scalar1=st[i][:, 0:1], scalar2=1.0 / 448.0,
+                                    op0=ALU.max, op1=ALU.mult)
 
         def r_scale(i):
             nc.vector.reciprocal(out=st[i][:, 16:17], in_=st[i][:, 8:9])
@@ -281,41 +286,41 @@ def tile_time2vec_kernel(tc, x, W, Pb, w, p, sine_w, cosine_w, out_0, out_1):
                                  scale=st[i][:, 16:17], saturate=False)
             nc.sync.dma_start(out=out_1[i * P:(i + 1) * P, :], in_=o8[i][:].bitcast(U8))
 
-        for h in range(NH):
-            nc.scalar.activation(out=pq[:, h * H:(h + 1) * H], in_=pbs[h][:], func=ACT.Copy, scale=INV2PI)
-        x_transpose(0)
-        x_copy(0)
         w_copy_vec(0, 0)
         w_copy_act(0, 0)
-        x_quant(0)
+        first_angle()
         w_copy_vec(1, 0)
         w_copy_act(1, 0)
-        first_angle()
         refine(0)
         w_quant(0, 0)
         w_copy_vec(0, 1)
+        x_transpose(0)
+        x_copy(0)
         w_copy_act(0, 1)
         w_quant(1, 0)
-        mm(0, (0,))
         w_copy_vec(1, 1)
         w_copy_act(1, 1)
+        x_quant(0)
+        mm(0, (0,))
+        nc.scalar.activation(out=pq[:, 0:H], in_=pbs[0][:], func=ACT.Copy, scale=INV2PI)
         refine(1)
         act(phs[:], phi, ACT.Copy, scale=INV2PI)
-        amplitude()
+        nc.scalar.activation(out=pq[:, H:N], in_=pbs[1][:], func=ACT.Copy, scale=INV2PI)
         w_quant(0, 1)
         w_quant(1, 1)
         x_transpose(1)
         x_transpose(2)
         mm(0, (1,))
         turns(0, 0)
+        turns(0, 1)
         x_copy(1)
         x_quant(1)
-        turns(0, 1)
         x_transpose(3)
         x_copy(2)
         x_quant(2)
         mm(1)
         x_transpose(4)
+        amplitude()
         x_copy(3)
         x_transpose(5)
 
@@ -326,9 +331,10 @@ def tile_time2vec_kernel(tc, x, W, Pb, w, p, sine_w, cosine_w, out_0, out_1):
             if 1 <= k <= NT:
                 sine(k - 1)
             if 2 <= k <= NT + 1:
-                row_amax(k - 2)
+                amax_periodic(k - 2)
             if 1 <= k <= NT:
                 periodic(k - 1)
+                amax_linear(k - 1)
             if k < NT:
                 linear(k)
                 frac(k)

@@ -173,11 +173,13 @@ def tile_time2vec_kernel(tc, x, W, Pb, w, p, sine_w, cosine_w, out_0, out_1):
 
         def w_copy_vec(g, h):
             cv = W_VEC_COLS
-            nc.vector.tensor_copy(out=wgrp[(g, h)][:, 0:cv, :], in_=wraw[(g, h)][:, :, 0:cv].rearrange("p j n -> p n j"))
+            nc.vector.tensor_copy(out=wgrp[(g, h)][:, 0:cv, :].rearrange("p (c i) j -> p c j i", i=4),
+                                  in_=wraw[(g, h)][:, :, 0:cv].rearrange("p j (c i) -> p c j i", i=4))
 
         def w_copy_act(g, h):
             cv = W_VEC_COLS
-            nc.scalar.copy(out=wgrp[(g, h)][:, cv:H, :], in_=wraw[(g, h)][:, :, cv:H].rearrange("p j n -> p n j"))
+            nc.scalar.copy(out=wgrp[(g, h)][:, cv:H, :].rearrange("p (c i) j -> p c j i", i=4),
+                           in_=wraw[(g, h)][:, :, cv:H].rearrange("p j (c i) -> p c j i", i=4))
 
         def w_quant(g, h):
             nc.vector.quantize_mx(

@@ -27,8 +27,8 @@ INV2PI = 1.0 / (2.0 * math.pi)
 TWOPI = 2.0 * math.pi
 START_A = 1.542
 START_B = 0.618
-W_VEC_COLS = 336
-CAST_VEC_COLS = (0, 0, 0, 0, 0, 640, 768, 1280)
+W_VEC_COLS = 368
+CAST_VEC_COLS = (0, 0, 0, 0, 0, 0, 1152, 2048)
 
 
 def tile_time2vec_kernel(tc, x, W, Pb, w, p, sine_w, cosine_w, out_0, out_1):
@@ -36,6 +36,7 @@ def tile_time2vec_kernel(tc, x, W, Pb, w, p, sine_w, cosine_w, out_0, out_1):
     with ExitStack() as ctx:
         const = ctx.enter_context(tc.tile_pool(name="const", bufs=1))
         xgp = ctx.enter_context(tc.tile_pool(name="xgp", bufs=3))
+        xip = ctx.enter_context(tc.tile_pool(name="xip", bufs=NT))
         ep = ctx.enter_context(tc.tile_pool(name="ep", bufs=3))
         op = ctx.enter_context(tc.tile_pool(name="op", bufs=8))
         o8p = ctx.enter_context(tc.tile_pool(name="o8p", bufs=3))
@@ -118,19 +119,21 @@ def tile_time2vec_kernel(tc, x, W, Pb, w, p, sine_w, cosine_w, out_0, out_1):
         nc.vector.tensor_copy(out=sc[:], in_=scb[:, 0:64:16])
         sgh = small("sgh")
         nc.vector.tensor_scalar(out=sgh[:], in0=sw, scalar1=0.0, scalar2=0.5, op0=ALU.is_ge, op1=ALU.subtract)
-        hv = small("hv", 2)
-        nc.vector.tensor_scalar(out=hv[:], in0=sc[:, 2:4], scalar1=sgh[:, 0:1], scalar2=None, op0=ALU.mult)
+        hv = small("hv", 3)
+        nc.vector.tensor_scalar(out=hv[:, 0:2], in0=sc[:, 2:4], scalar1=sgh[:, 0:1], scalar2=None, op0=ALU.mult)
         b2 = small("b2")
         nc.vector.tensor_scalar(out=b2[:], in0=hv[:, 1:2], scalar1=hv[:, 1:2], scalar2=1e-30, op0=ALU.mult, op1=ALU.max)
         q4 = small("q4")
         nc.vector.tensor_scalar(out=q4[:], in0=hv[:, 0:1], scalar1=hv[:, 0:1], scalar2=b2[:, 0:1], op0=ALU.mult,
                                 op1=ALU.add)
+        nc.vector.tensor_scalar(out=hv[:, 2:3], in0=hv[:, 0:1], scalar1=-1.0, scalar2=None, op0=ALU.mult)
+        q4s = small("q4s")
+        nc.vector.tensor_scalar(out=q4s[:], in0=q4[:], scalar1=sgh[:, 0:1], scalar2=4.0, op0=ALU.mult, op1=ALU.mult)
         rn2 = small("rn2")
         nc.gpsimd.tensor_tensor(out=rn2[:], in0=q4[:], in1=mhalf[:], op=ALU.pow)
-        cs = small("cs", 2)
-        c0, s0 = cs[:, 0:1], cs[:, 1:2]
+        cs = small("cs", 3)
+        c0, s0, nc0 = cs[:, 0:1], cs[:, 1:2], cs[:, 2:3]
         slope = small("slope")
-        nc0 = small("nc0")
         angs = [small("ang%d" % it) for it in range(3)]
         phs = small("phs")
         amp = small("amp")
@@ -147,7 +150,6 @@ def tile_time2vec_kernel(tc, x, W, Pb, w, p, sine_w, cosine_w, out_0, out_1):
         def first_angle():
             act(cs[:], hv[:], ACT.Identity, scale=rn2[:, 0:1])
             act(slope[:], c0, ACT.Identity, scale=-START_B, bias=start_a[:, 0:1])
-            act(nc0[:], c0, ACT.Copy, scale=-1.0)
             act(angs[0][:], slope[:], ACT.Identity, scale=s0)
 
         def sin_cos(it):
@@ -162,14 +164,11 @@ def tile_time2vec_kernel(tc, x, W, Pb, w, p, sine_w, cosine_w, out_0, out_1):
         def refine(it):
             sn, cn = sin_cos(it)
             t1 = small("t1_%d" % it)
-            act(t1[:], sn[:], ACT.Identity, scale=nc0[:, 0:1], bias=angs[it][:, 0:1])
+            act(t1[:], sn[:], ACT.Identity, scale=nc0, bias=angs[it][:, 0:1])
             act(angs[it + 1][:], cn[:], ACT.Identity, scale=s0, bias=t1[:, 0:1])
 
         def amplitude():
-            sn, cn = sin_cos(2)
-            u1 = small("u1")
-            act(u1[:], sn[:], ACT.Identity, scale=cw)
-            act(amp[:], cn[:], ACT.Identity, scale=sw, bias=u1[:, 0:1])
+            act(amp[:], q4s[:], ACT.Identity, scale=rn2[:, 0:1])
 
         def w_copy_vec(g, h):
             cv = W_VEC_COLS
@@ -198,7 +197,7 @@ def tile_time2vec_kernel(tc, x, W, Pb, w, p, sine_w, cosine_w, out_0, out_1):
                     nc.tensor.transpose(xt[i][:, g, u, :], words[:, 256 * g + u:256 * (g + 1):2], ident[:])
 
         def x_copy(i):
-            xg[i] = xgp.tile([P, 4 * NG * P], BF16, name="xg", tag="xg", align_bytes=64)
+            xg[i] = xip.tile([P, 4 * NG * P], BF16, name="xg", tag="xg", align_bytes=64)
             nc.scalar.copy(
                 out=xg[i][:].bitcast(F32).rearrange("p (g r u) -> p g r u", g=NG, u=2),
                 in_=xt[i][:].rearrange("p g u r -> p g r u"),
@@ -242,11 +241,7 @@ def tile_time2vec_kernel(tc, x, W, Pb, w, p, sine_w, cosine_w, out_0, out_1):
             nc.scalar.activation(out=s[i][:], in_=fr[i][:], func=ACT.Sin, bias=phi, scale=TWOPI)
 
         def periodic(i):
-            if i == NT - 1:
-                nc.vector.tensor_scalar(out=o[i][:, N:2 * N], in0=s[i][:], scalar1=amp[:, 0:1], scalar2=None,
-                                        op0=ALU.mult)
-            else:
-                nc.scalar.activation(out=o[i][:, N:2 * N], in_=s[i][:], func=ACT.Identity, scale=amp[:, 0:1])
+            nc.scalar.activation(out=o[i][:, N:2 * N], in_=s[i][:], func=ACT.Identity, scale=amp[:, 0:1])
             nc.sync.dma_start(out=out_0[i * P:(i + 1) * P, N:2 * N], in_=o[i][:, N:2 * N])
 
         def linear(i):
@@ -284,8 +279,9 @@ def tile_time2vec_kernel(tc, x, W, Pb, w, p, sine_w, cosine_w, out_0, out_1):
 
         def cast_act(i):
             cc = 2 * N - CAST_VEC_COLS[i]
-            nc.scalar.activation(out=o8[i][:, 0:cc], in_=o[i][:, 0:cc], func=ACT.Identity, bias=zero[:, 0:1],
-                                 scale=st[i][:, 16:17], saturate=False)
+            if cc > 0:
+                nc.scalar.activation(out=o8[i][:, 0:cc], in_=o[i][:, 0:cc], func=ACT.Identity, bias=zero[:, 0:1],
+                                     scale=st[i][:, 16:17], saturate=False)
             nc.sync.dma_start(out=out_1[i * P:(i + 1) * P, :], in_=o8[i][:].bitcast(U8))
 
         w_copy_vec(0, 0)
@@ -303,6 +299,7 @@ def tile_time2vec_kernel(tc, x, W, Pb, w, p, sine_w, cosine_w, out_0, out_1):
         w_copy_vec(1, 1)
         w_copy_act(1, 1)
         x_quant(0)
+        x_transpose(1)
         mm(0, (0,))
         nc.scalar.activation(out=pq[:, 0:H], in_=pbs[0][:], func=ACT.Copy, scale=INV2PI)
         refine(1)
@@ -310,9 +307,8 @@ def tile_time2vec_kernel(tc, x, W, Pb, w, p, sine_w, cosine_w, out_0, out_1):
         nc.scalar.activation(out=pq[:, H:N], in_=pbs[1][:], func=ACT.Copy, scale=INV2PI)
         w_quant(0, 1)
         w_quant(1, 1)
-        x_transpose(1)
-        x_transpose(2)
         mm(0, (1,))
+        x_transpose(2)
         turns(0, 0)
         turns(0, 1)
         x_copy(1)
@@ -350,9 +346,10 @@ def tile_time2vec_kernel(tc, x, W, Pb, w, p, sine_w, cosine_w, out_0, out_1):
                 cast_vec(k - 3)
             if 2 <= k <= NT + 1:
                 r_scale(k - 2)
-            if k >= 1 and k + 3 < NT:
-                x_copy(k + 3)
-            if k >= 1 and k + 5 < NT:
-                x_transpose(k + 5)
+            if k in (1, 2):
+                for i in (2 * k + 2, 2 * k + 3):
+                    x_copy(i)
+                    if i + 2 < NT:
+                        x_transpose(i + 2)
             if k >= 3:
                 cast_act(k - 3)

@@ -28,7 +28,7 @@ TWOPI = 2.0 * math.pi
 START_A = 1.542
 START_B = 0.618
 W_VEC_COLS = 368
-CAST_VEC_COLS = (0, 0, 0, 0, 0, 0, 1152, 2048)
+TAIL_SPLIT = 896
 
 
 def tile_time2vec_kernel(tc, x, W, Pb, w, p, sine_w, cosine_w, out_0, out_1):
@@ -90,17 +90,16 @@ def tile_time2vec_kernel(tc, x, W, Pb, w, p, sine_w, cosine_w, out_0, out_1):
         for g in range(NG):
             for h in range(NH):
                 wgrp[(g, h)] = const.tile([P, H, 4], BF16, name="wgrp%d%d" % (g, h), align_bytes=64)
-        pq = const.tile([P, N], F32, name="pq")
-        sc = const.tile([P, 4], F32, name="sc")
+        pb = const.tile([P, N], BF16, name="pb")
+        sc = const.tile([P, 5], F32, name="sc")
         w_t, p_t, sw, cw = sc[:, 0:1], sc[:, 1:2], sc[:, 2:3], sc[:, 3:4]
 
         ctx.enter_context(tc.manual_schedule())
 
-        pbs = []
+        pbank = accp.tile([P, N], BF16, name="pbank", tag="acc")
         for h in range(NH):
-            pb = accp.tile([P, H], F32, name="pb%d" % h, tag="acc")
-            nc.tensor.matmul(pb[:], lhsT=ones[:], rhs=zp[:, h * H:(h + 1) * H], start=True, stop=True)
-            pbs.append(pb)
+            nc.tensor.matmul(pbank[:, h * H:(h + 1) * H], lhsT=ones[:], rhs=zp[:, h * H:(h + 1) * H], start=True,
+                             stop=True)
 
         def small(name, cols=1):
             return const.tile([P, cols], F32, name=name)
@@ -116,29 +115,6 @@ def tile_time2vec_kernel(tc, x, W, Pb, w, p, sine_w, cosine_w, out_0, out_1):
         start_a = small("start_a")
         gts(start_a[:], zero[:], 0.0, START_A, ALU.mult, ALU.add)
 
-        nc.vector.tensor_copy(out=sc[:], in_=scb[:, 0:64:16])
-        sgh = small("sgh")
-        nc.vector.tensor_scalar(out=sgh[:], in0=sw, scalar1=0.0, scalar2=0.5, op0=ALU.is_ge, op1=ALU.subtract)
-        hv = small("hv", 3)
-        nc.vector.tensor_scalar(out=hv[:, 0:2], in0=sc[:, 2:4], scalar1=sgh[:, 0:1], scalar2=None, op0=ALU.mult)
-        b2 = small("b2")
-        nc.vector.tensor_scalar(out=b2[:], in0=hv[:, 1:2], scalar1=hv[:, 1:2], scalar2=1e-30, op0=ALU.mult, op1=ALU.max)
-        q4 = small("q4")
-        nc.vector.tensor_scalar(out=q4[:], in0=hv[:, 0:1], scalar1=hv[:, 0:1], scalar2=b2[:, 0:1], op0=ALU.mult,
-                                op1=ALU.add)
-        nc.vector.tensor_scalar(out=hv[:, 2:3], in0=hv[:, 0:1], scalar1=-1.0, scalar2=None, op0=ALU.mult)
-        q4s = small("q4s")
-        nc.vector.tensor_scalar(out=q4s[:], in0=q4[:], scalar1=sgh[:, 0:1], scalar2=4.0, op0=ALU.mult, op1=ALU.mult)
-        rn2 = small("rn2")
-        nc.gpsimd.tensor_tensor(out=rn2[:], in0=q4[:], in1=mhalf[:], op=ALU.pow)
-        cs = small("cs", 3)
-        c0, s0, nc0 = cs[:, 0:1], cs[:, 1:2], cs[:, 2:3]
-        slope = small("slope")
-        angs = [small("ang%d" % it) for it in range(3)]
-        phs = small("phs")
-        amp = small("amp")
-        phi = angs[2][:, 0:1]
-
         def act(out, in_, func, scale=None, bias=None):
             if scale is None and bias is None:
                 nc.scalar.activation(out=out, in_=in_, func=func)
@@ -147,28 +123,52 @@ def tile_time2vec_kernel(tc, x, W, Pb, w, p, sine_w, cosine_w, out_0, out_1):
             else:
                 nc.scalar.activation(out=out, in_=in_, func=func, scale=scale, bias=bias)
 
-        def first_angle():
+        sch = small("sch", 2)
+        nc.vector.tensor_scalar(out=sch[:], in0=scb[:, 32:64:16], scalar1=0.5, scalar2=None, op0=ALU.mult)
+        b2 = small("b2")
+        nc.vector.tensor_scalar(out=b2[:], in0=sch[:, 1:2], scalar1=sch[:, 1:2], scalar2=1e-30, op0=ALU.mult,
+                                op1=ALU.max)
+        sgh = small("sgh")
+        nc.vector.tensor_scalar(out=sgh[:], in0=sch[:, 0:1], scalar1=0.0, scalar2=0.5, op0=ALU.is_ge, op1=ALU.subtract)
+        q4 = small("q4")
+        nc.vector.tensor_scalar(out=q4[:], in0=sch[:, 0:1], scalar1=sch[:, 0:1], scalar2=b2[:, 0:1], op0=ALU.mult,
+                                op1=ALU.add)
+        rn2 = small("rn2")
+        nc.gpsimd.tensor_tensor(out=rn2[:], in0=q4[:], in1=mhalf[:], op=ALU.pow)
+        nc.scalar.copy(out=sc[:, 0:4], in_=scb[:, 0:64:16])
+        act(sc[:, 4:5], scb[:, 32:33], ACT.Copy, scale=-1.0)
+        hv = small("hv", 3)
+        act(hv[:], sc[:, 2:5], ACT.Identity, scale=sgh[:, 0:1])
+        cs = small("cs", 3)
+        c0, s0, nc0 = cs[:, 0:1], cs[:, 1:2], cs[:, 2:3]
+        slope = small("slope")
+        angs = [small("ang%d" % it) for it in range(3)]
+        t1s = [small("t1_%d" % it) for it in range(2)]
+        cns = [small("cn%d" % it) for it in range(2)]
+        phs = small("phs")
+        u1 = small("u1")
+        amp = small("amp")
+        phi = angs[2][:, 0:1]
+
+        def unit_vector():
             act(cs[:], hv[:], ACT.Identity, scale=rn2[:, 0:1])
+
+        def start_slope():
             act(slope[:], c0, ACT.Identity, scale=-START_B, bias=start_a[:, 0:1])
+
+        def start_angle():
             act(angs[0][:], slope[:], ACT.Identity, scale=s0)
 
-        def sin_cos(it):
+        def refine_terms(it):
             ab = small("ab%d" % it)
             sn = small("sn%d" % it)
-            cn = small("cn%d" % it)
             act(ab[:], angs[it][:], ACT.Abs)
             act(sn[:], angs[it][:], ACT.Sin)
-            act(cn[:], ab[:], ACT.Sin, scale=-1.0, bias=halfpi[:, 0:1])
-            return sn, cn
+            act(cns[it][:], ab[:], ACT.Sin, scale=-1.0, bias=halfpi[:, 0:1])
+            act(t1s[it][:], sn[:], ACT.Identity, scale=nc0, bias=angs[it][:, 0:1])
 
-        def refine(it):
-            sn, cn = sin_cos(it)
-            t1 = small("t1_%d" % it)
-            act(t1[:], sn[:], ACT.Identity, scale=nc0, bias=angs[it][:, 0:1])
-            act(angs[it + 1][:], cn[:], ACT.Identity, scale=s0, bias=t1[:, 0:1])
-
-        def amplitude():
-            act(amp[:], q4s[:], ACT.Identity, scale=rn2[:, 0:1])
+        def refine_sum(it):
+            act(angs[it + 1][:], cns[it][:], ACT.Identity, scale=s0, bias=t1s[it][:, 0:1])
 
         def w_copy_vec(g, h):
             cv = W_VEC_COLS
@@ -227,18 +227,22 @@ def tile_time2vec_kernel(tc, x, W, Pb, w, p, sine_w, cosine_w, out_0, out_1):
                 v[i] = ep.tile([P, N], F32, name="v", tag="v")
                 n[i] = ep.tile([P, N], I32, name="n", tag="n")
             cols = slice(h * H, (h + 1) * H)
-            nc.vector.scalar_tensor_tensor(out=v[i][:, cols], in0=acc[(i, h)][:], scalar=INV2PI, in1=pq[:, cols],
-                                           op0=ALU.mult, op1=ALU.add)
-            nc.gpsimd.tensor_scalar(out=n[i][:, cols], in0=v[i][:, cols], scalar1=1.0, scalar2=phs[:, 0:1],
-                                    op0=ALU.mult, op1=ALU.add)
+            nc.vector.tensor_tensor(out=v[i][:, cols], in0=acc[(i, h)][:], in1=pb[:, cols], op=ALU.add)
+            if i > 0:
+                nc.gpsimd.tensor_scalar(out=n[i][:, cols], in0=v[i][:, cols], scalar1=INV2PI, scalar2=phs[:, 0:1],
+                                        op0=ALU.mult, op1=ALU.add)
+            elif h == 1:
+                nc.vector.tensor_scalar(out=n[i][:], in0=v[i][:], scalar1=INV2PI, scalar2=phs[:, 0:1], op0=ALU.mult,
+                                        op1=ALU.add)
 
         def frac(i):
             fr[i] = ep.tile([P, N], F32, name="fr", tag="fr")
-            nc.vector.tensor_tensor(out=fr[i][:], in0=v[i][:], in1=n[i][:], op=ALU.subtract)
+            nc.vector.scalar_tensor_tensor(out=fr[i][:], in0=n[i][:], scalar=-TWOPI, in1=v[i][:], op0=ALU.mult,
+                                           op1=ALU.add)
 
         def sine(i):
             s[i] = ep.tile([P, N], F32, name="s", tag="s")
-            nc.scalar.activation(out=s[i][:], in_=fr[i][:], func=ACT.Sin, bias=phi, scale=TWOPI)
+            nc.scalar.activation(out=s[i][:], in_=fr[i][:], func=ACT.Sin, bias=phi, scale=1.0)
 
         def periodic(i):
             nc.scalar.activation(out=o[i][:, N:2 * N], in_=s[i][:], func=ACT.Identity, scale=amp[:, 0:1])
@@ -270,41 +274,46 @@ def tile_time2vec_kernel(tc, x, W, Pb, w, p, sine_w, cosine_w, out_0, out_1):
 
         o8 = {}
 
-        def cast_vec(i):
+        def cast_tile(i):
             o8[i] = o8p.tile([P, 2 * N], FP8, name="o8", tag="o8")
-            cc = 2 * N - CAST_VEC_COLS[i]
-            if cc < 2 * N:
-                nc.vector.tensor_scalar(out=o8[i][:, cc:2 * N], in0=o[i][:, cc:2 * N], scalar1=st[i][:, 16:17],
-                                        scalar2=None, op0=ALU.mult, saturate=False)
 
-        def cast_act(i):
-            cc = 2 * N - CAST_VEC_COLS[i]
-            if cc > 0:
-                nc.scalar.activation(out=o8[i][:, 0:cc], in_=o[i][:, 0:cc], func=ACT.Identity, bias=zero[:, 0:1],
-                                     scale=st[i][:, 16:17], saturate=False)
+        def cast_vec(i, lo, hi):
+            nc.vector.tensor_scalar(out=o8[i][:, lo:hi], in0=o[i][:, lo:hi], scalar1=st[i][:, 16:17], scalar2=None,
+                                    op0=ALU.mult, saturate=False)
+
+        def cast_act(i, hi):
+            nc.scalar.activation(out=o8[i][:, 0:hi], in_=o[i][:, 0:hi], func=ACT.Identity, bias=zero[:, 0:1],
+                                 scale=st[i][:, 16:17], saturate=False)
+
+        def store_bytes(i):
             nc.sync.dma_start(out=out_1[i * P:(i + 1) * P, :], in_=o8[i][:].bitcast(U8))
 
         w_copy_vec(0, 0)
         w_copy_act(0, 0)
-        first_angle()
+        unit_vector()
         w_copy_vec(1, 0)
         w_copy_act(1, 0)
-        refine(0)
+        start_slope()
         w_quant(0, 0)
         w_copy_vec(0, 1)
         x_transpose(0)
         x_copy(0)
+        start_angle()
         w_copy_act(0, 1)
+        refine_terms(0)
         w_quant(1, 0)
         w_copy_vec(1, 1)
         w_copy_act(1, 1)
+        refine_sum(0)
         x_quant(0)
         x_transpose(1)
         mm(0, (0,))
-        nc.scalar.activation(out=pq[:, 0:H], in_=pbs[0][:], func=ACT.Copy, scale=INV2PI)
-        refine(1)
+        nc.scalar.copy(out=pb[:], in_=pbank[:])
+        refine_terms(1)
+        act(u1[:], c0, ACT.Identity, scale=sw)
+        refine_sum(1)
+        act(amp[:], s0, ACT.Identity, scale=cw, bias=u1[:, 0:1])
         act(phs[:], phi, ACT.Copy, scale=INV2PI)
-        nc.scalar.activation(out=pq[:, H:N], in_=pbs[1][:], func=ACT.Copy, scale=INV2PI)
         w_quant(0, 1)
         w_quant(1, 1)
         mm(0, (1,))
@@ -318,33 +327,28 @@ def tile_time2vec_kernel(tc, x, W, Pb, w, p, sine_w, cosine_w, out_0, out_1):
         x_quant(2)
         mm(1)
         x_transpose(4)
-        amplitude()
         x_copy(3)
         x_transpose(5)
 
-        for k in range(NT + 3):
-            if 1 <= k < NT:
+        for k in range(NT):
+            if k >= 1:
                 turns(k, 0)
                 turns(k, 1)
-            if 1 <= k <= NT:
                 sine(k - 1)
-            if 2 <= k <= NT + 1:
+            if k >= 2:
                 amax_periodic(k - 2)
-            if 1 <= k <= NT:
+            if k >= 1:
                 periodic(k - 1)
                 amax_linear(k - 1)
-            if k < NT:
-                linear(k)
-                frac(k)
-            if 2 <= k <= NT + 1:
+            linear(k)
+            if k >= 2:
                 q_scale(k - 2)
             if 3 <= k + 2 < NT:
                 x_quant(k + 2)
             if k + 2 < NT:
                 mm(k + 2)
-            if k >= 3:
-                cast_vec(k - 3)
-            if 2 <= k <= NT + 1:
+            frac(k)
+            if k >= 2:
                 r_scale(k - 2)
             if k in (1, 2):
                 for i in (2 * k + 2, 2 * k + 3):
@@ -352,4 +356,27 @@ def tile_time2vec_kernel(tc, x, W, Pb, w, p, sine_w, cosine_w, out_0, out_1):
                     if i + 2 < NT:
                         x_transpose(i + 2)
             if k >= 3:
-                cast_act(k - 3)
+                cast_tile(k - 3)
+                cast_act(k - 3, 2 * N)
+                store_bytes(k - 3)
+
+        a, b, c = NT - 3, NT - 2, NT - 1
+        sine(c)
+        amax_periodic(b)
+        periodic(c)
+        amax_linear(c)
+        q_scale(b)
+        cast_tile(a)
+        cast_act(a, 2 * N)
+        store_bytes(a)
+        amax_periodic(c)
+        r_scale(b)
+        q_scale(c)
+        cast_tile(b)
+        cast_vec(b, TAIL_SPLIT, 2 * N)
+        r_scale(c)
+        cast_act(b, TAIL_SPLIT)
+        store_bytes(b)
+        cast_tile(c)
+        cast_vec(c, 0, 2 * N)
+        store_bytes(c)

@@ -248,6 +248,17 @@ def tile_time2vec_kernel(tc, x, W, Pb, w, p, sine_w, cosine_w, out_0, out_1):
             nc.scalar.activation(out=o[i][:, N:2 * N], in_=s[i][:], func=ACT.Identity, scale=amp[:, 0:1])
             nc.sync.dma_start(out=out_0[i * P:(i + 1) * P, N:2 * N], in_=o[i][:, N:2 * N])
 
+        def periodic_part(i, lo, hi, pool):
+            if pool:
+                nc.gpsimd.tensor_scalar(out=o[i][:, N + lo:N + hi], in0=s[i][:, lo:hi], scalar1=amp[:, 0:1], scalar2=0.0,
+                                        op0=ALU.mult, op1=ALU.add)
+            else:
+                nc.scalar.activation(out=o[i][:, N + lo:N + hi], in_=s[i][:, lo:hi], func=ACT.Identity,
+                                     scale=amp[:, 0:1])
+
+        def store_periodic(i):
+            nc.sync.dma_start(out=out_0[i * P:(i + 1) * P, N:2 * N], in_=o[i][:, N:2 * N])
+
         def linear(i):
             o[i] = op.tile([P, 2 * N], F32, name="o", tag="o")
             for h in range(2):
@@ -335,6 +346,15 @@ def tile_time2vec_kernel(tc, x, W, Pb, w, p, sine_w, cosine_w, out_0, out_1):
                 turns(k, 0)
                 turns(k, 1)
                 sine(k - 1)
+            if k in (1, 2):
+                for i in (2 * k + 2, 2 * k + 3):
+                    x_copy(i)
+                    if i + 2 < NT:
+                        x_transpose(i + 2)
+            if k >= 3:
+                cast_tile(k - 3)
+                cast_act(k - 3, 2 * N)
+                store_bytes(k - 3)
             if k >= 2:
                 amax_periodic(k - 2)
             if k >= 1:
@@ -350,20 +370,13 @@ def tile_time2vec_kernel(tc, x, W, Pb, w, p, sine_w, cosine_w, out_0, out_1):
             frac(k)
             if k >= 2:
                 r_scale(k - 2)
-            if k in (1, 2):
-                for i in (2 * k + 2, 2 * k + 3):
-                    x_copy(i)
-                    if i + 2 < NT:
-                        x_transpose(i + 2)
-            if k >= 3:
-                cast_tile(k - 3)
-                cast_act(k - 3, 2 * N)
-                store_bytes(k - 3)
 
         a, b, c = NT - 3, NT - 2, NT - 1
         sine(c)
         amax_periodic(b)
-        periodic(c)
+        periodic_part(c, 0, H, True)
+        periodic_part(c, H, N, False)
+        store_periodic(c)
         amax_linear(c)
         q_scale(b)
         cast_tile(a)

@@ -29,6 +29,7 @@ START_A = 1.542
 START_B = 0.618
 W_VEC_COLS = 368
 TAIL_SPLIT = 896
+TAIL_PIECE = 576
 
 
 def tile_time2vec_kernel(tc, x, W, Pb, w, p, sine_w, cosine_w, out_0, out_1):
@@ -261,7 +262,9 @@ def tile_time2vec_kernel(tc, x, W, Pb, w, p, sine_w, cosine_w, out_0, out_1):
 
         def linear(i):
             o[i] = op.tile([P, 2 * N], F32, name="o", tag="o")
-            for h in range(2):
+            if i == 0:
+                nc.scalar.activation(out=o[i][:, 0:N], in_=xs[i][:], func=ACT.Identity, bias=p_t, scale=w_t)
+            for h in range(2 if i > 0 else 0):
                 cols = slice(h * H, (h + 1) * H)
                 nc.gpsimd.tensor_scalar(out=o[i][:, cols], in0=xs[i][:, cols], scalar1=w_t, scalar2=p_t,
                                         op0=ALU.mult, op1=ALU.add)
@@ -386,8 +389,9 @@ def tile_time2vec_kernel(tc, x, W, Pb, w, p, sine_w, cosine_w, out_0, out_1):
         r_scale(b)
         q_scale(c)
         cast_tile(b)
-        cast_vec(b, TAIL_SPLIT, 2 * N)
+        cast_vec(b, TAIL_SPLIT, TAIL_SPLIT + TAIL_PIECE)
         r_scale(c)
+        cast_vec(b, TAIL_SPLIT + TAIL_PIECE, 2 * N)
         cast_act(b, TAIL_SPLIT)
         store_bytes(b)
         cast_tile(c)

@@ -311,6 +311,9 @@ def tile_time2vec_kernel(tc, x, W, Pb, w, p, sine_w, cosine_w, out_0, out_1):
         w_quant(0, 0)
         w_copy_vec(0, 1)
         x_transpose(0)
+        warm_bank = accp.tile([P, H], F32, name="warm_bank", tag="acc")
+        for rep_i in range(4):
+            nc.tensor.matmul(warm_bank[:], lhsT=ones[:], rhs=zp[:, 0:H], start=True, stop=True)
         x_copy(0)
         start_angle()
         w_copy_act(0, 1)

@@ -93,6 +93,7 @@ def tile_time2vec_kernel(tc, x, W, Pb, w, p, sine_w, cosine_w, out_0, out_1):
                 wgrp[(g, h)] = const.tile([P, H, 4], BF16, name="wgrp%d%d" % (g, h), align_bytes=64)
         pb = const.tile([P, N], BF16, name="pb")
         sc = const.tile([P, 5], F32, name="sc")
+        o_all = const.tile([P, NT * 2 * N], F32, name="o_all")
         w_t, p_t, sw, cw = sc[:, 0:1], sc[:, 1:2], sc[:, 2:3], sc[:, 3:4]
 
         ctx.enter_context(tc.manual_schedule())
@@ -261,7 +262,7 @@ def tile_time2vec_kernel(tc, x, W, Pb, w, p, sine_w, cosine_w, out_0, out_1):
             nc.sync.dma_start(out=out_0[i * P:(i + 1) * P, N:2 * N], in_=o[i][:, N:2 * N])
 
         def linear(i):
-            o[i] = op.tile([P, 2 * N], F32, name="o", tag="o")
+            o[i] = o_all[:, i * 2 * N:(i + 1) * 2 * N]
             if i == 0:
                 nc.scalar.activation(out=o[i][:, 0:N], in_=xs[i][:], func=ACT.Identity, bias=p_t, scale=w_t)
             for h in range(2 if i > 0 else 0):

import math
from contextlib import ExitStack

import concourse.mybir as mybir
from concourse.masks import make_identity

FLOPS = 2 * 1024 * 1024 * 1024

F32 = mybir.dt.float32
BF16 = mybir.dt.bfloat16
I32 = mybir.dt.int32
U32 = mybir.dt.uint32
U8 = mybir.dt.uint8
FP8 = mybir.dt.float8_e4m3fn
FP8X4 = mybir.dt.float8_e4m3fn_x4
ALU = mybir.AluOpType
ACT = mybir.ActivationFunctionType
AX = mybir.AxisListType

P = 128
B, K, N = 1024, 1024, 1024
NT = B // P
NG = K // 512
NH = N // 512
H = 512
INV2PI = 1.0 / (2.0 * math.pi)
TWOPI = 2.0 * math.pi
START_A = 1.542
START_B = 0.618
W_VEC_COLS = 368
TAIL_SPLIT = 896
TAIL_PIECE = 576


def tile_time2vec_kernel(tc, x, W, Pb, w, p, sine_w, cosine_w, out_0, out_1):
    nc = tc.nc
    with ExitStack() as ctx:
        const = ctx.enter_context(tc.tile_pool(name="const", bufs=1))
        xgp = ctx.enter_context(tc.tile_pool(name="xgp", bufs=3))
        xip = ctx.enter_context(tc.tile_pool(name="xip", bufs=NT))
        ep = ctx.enter_context(tc.tile_pool(name="ep", bufs=3))
        op = ctx.enter_context(tc.tile_pool(name="op", bufs=8))
        o8p = ctx.enter_context(tc.tile_pool(name="o8p", bufs=3))
        accp = ctx.enter_context(tc.psum_pool(name="accp", bufs=6))
        xtp = ctx.enter_context(tc.psum_pool(name="xtp", bufs=2))

        xs = {}
        wraw = {}

        def load_x(i):
            t = const.tile([P, K], BF16, name="x%d" % i)
            nc.sync.dma_start(out=t[:], in_=x[i * P:(i + 1) * P, :])
            xs[i] = t

        def load_w(g, h):
            t = const.tile([P, 4, H], BF16, name="wraw%d%d" % (g, h))
            nc.sync.dma_start(
                out=t[:],
                in_=W[g * 512:(g + 1) * 512, h * H:(h + 1) * H].rearrange("(p j) n -> p j n", j=4),
            )
            wraw[(g, h)] = t

        scb = const.tile([P, 64], BF16, name="scb")
        for j, sc_in in enumerate((w, p, sine_w, cosine_w)):
            nc.sync.dma_start(out=scb[:, 16 * j:16 * j + 1], in_=sc_in.partition_broadcast(P))
        zp = const.tile([P, N], BF16, name="zp")
        nc.vector.memset(zp[:], 0.0)
        ones = const.tile([P, P], BF16, name="ones")
        nc.vector.memset(ones[:], 1.0)
        load_w(0, 0)
        nc.sync.dma_start(out=zp[0:1, :], in_=Pb.rearrange("(o n) -> o n", o=1))
        load_w(1, 0)
        load_x(0)
        load_w(0, 1)
        load_w(1, 1)
        for i in range(1, NT):
            load_x(i)

        zero = const.tile([P, 1], F32, name="zero")
        nc.gpsimd.memset(zero[:], 0.0)
        mhalf = const.tile([P, 1], F32, name="mhalf")
        nc.gpsimd.memset(mhalf[:], -0.5)
        ident = const.tile([P, P], F32, name="ident")
        make_identity(nc, ident[:])
        warm = const.tile([P, 1], F32, name="warm")
        nc.scalar.activation(out=warm[:], in_=zero[:], func=ACT.Sin)

        wcodes = const.tile([P, NG, N], U32, name="wcodes", align_bytes=64)
        wscales = const.tile([P, NG, N], U8, name="wscales", align_bytes=64)
        wgrp = {}
        for g in range(NG):
            for h in range(NH):
                wgrp[(g, h)] = const.tile([P, H, 4], BF16, name="wgrp%d%d" % (g, h), align_bytes=64)
        pb = const.tile([P, N], BF16, name="pb")
        sc = const.tile([P, 5], F32, name="sc")
        o_all = const.tile([P, NT * 2 * N], F32, name="o_all")
        w_t, p_t, sw, cw = sc[:, 0:1], sc[:, 1:2], sc[:, 2:3], sc[:, 3:4]

        ctx.enter_context(tc.manual_schedule())

        pbank = accp.tile([P, N], BF16, name="pbank", tag="acc")
        for h in range(NH):
            nc.tensor.matmul(pbank[:, h * H:(h + 1) * H], lhsT=ones[:], rhs=zp[:, h * H:(h + 1) * H], start=True,
                             stop=True)

        def small(name, cols=1):
            return const.tile([P, cols], F32, name=name)

        def gts(out, in0, s1, s2, op0, op1=None):
            if op1 is None:
                nc.gpsimd.tensor_scalar(out=out, in0=in0, scalar1=s1, scalar2=None, op0=op0)
            else:
                nc.gpsimd.tensor_scalar(out=out, in0=in0, scalar1=s1, scalar2=s2, op0=op0, op1=op1)

        halfpi = small("halfpi")
        gts(halfpi[:], zero[:], 0.0, 0.5 * math.pi, ALU.mult, ALU.add)
        start_a = small("start_a")
        gts(start_a[:], zero[:], 0.0, START_A, ALU.mult, ALU.add)

        def act(out, in_, func, scale=None, bias=None):
            if scale is None and bias is None:
                nc.scalar.activation(out=out, in_=in_, func=func)
            elif bias is None:
                nc.scalar.activation(out=out, in_=in_, func=func, scale=scale)
            else:
                nc.scalar.activation(out=out, in_=in_, func=func, scale=scale, bias=bias)

        sch = small("sch", 2)
        nc.vector.tensor_scalar(out=sch[:], in0=scb[:, 32:64:16], scalar1=0.5, scalar2=None, op0=ALU.mult)
        b2 = small("b2")
        nc.vector.tensor_scalar(out=b2[:], in0=sch[:, 1:2], scalar1=sch[:, 1:2], scalar2=1e-30, op0=ALU.mult,
                                op1=ALU.max)
        sgh = small("sgh")
        nc.vector.tensor_scalar(out=sgh[:], in0=sch[:, 0:1], scalar1=0.0, scalar2=0.5, op0=ALU.is_ge, op1=ALU.subtract)
        q4 = small("q4")
        nc.vector.tensor_scalar(out=q4[:], in0=sch[:, 0:1], scalar1=sch[:, 0:1], scalar2=b2[:, 0:1], op0=ALU.mult,
                                op1=ALU.add)
        rn2 = small("rn2")
        nc.gpsimd.tensor_tensor(out=rn2[:], in0=q4[:], in1=mhalf[:], op=ALU.pow)
        nc.scalar.copy(out=sc[:, 0:4], in_=scb[:, 0:64:16])
        act(sc[:, 4:5], scb[:, 32:33], ACT.Copy, scale=-1.0)
        hv = small("hv", 3)
        act(hv[:], sc[:, 2:5], ACT.Identity, scale=sgh[:, 0:1])
        cs = small("cs", 3)
        c0, s0, nc0 = cs[:, 0:1], cs[:, 1:2], cs[:, 2:3]
        slope = small("slope")
        angs = [small("ang%d" % it) for it in range(3)]
        t1s = [small("t1_%d" % it) for it in range(2)]
        cns = [small("cn%d" % it) for it in range(2)]
        phs = small("phs")
        u1 = small("u1")
        amp = small("amp")
        phi = angs[2][:, 0:1]

        def unit_vector():
            act(cs[:], hv[:], ACT.Identity, scale=rn2[:, 0:1])

        def start_slope():
            act(slope[:], c0, ACT.Identity, scale=-START_B, bias=start_a[:, 0:1])

        def start_angle():
            act(angs[0][:], slope[:], ACT.Identity, scale=s0)

        def refine_terms(it):
            ab = small("ab%d" % it)
            sn = small("sn%d" % it)
            act(ab[:], angs[it][:], ACT.Abs)
            act(sn[:], angs[it][:], ACT.Sin)
            act(cns[it][:], ab[:], ACT.Sin, scale=-1.0, bias=halfpi[:, 0:1])
            act(t1s[it][:], sn[:], ACT.Identity, scale=nc0, bias=angs[it][:, 0:1])

        def refine_sum(it):
            act(angs[it + 1][:], cns[it][:], ACT.Identity, scale=s0, bias=t1s[it][:, 0:1])

        def w_copy_vec(g, h):
            cv = W_VEC_COLS
            nc.vector.tensor_copy(out=wgrp[(g, h)][:, 0:cv, :].rearrange("p (c i) j -> p c j i", i=4),
                                  in_=wraw[(g, h)][:, :, 0:cv].rearrange("p j (c i) -> p c j i", i=4))

        def w_copy_act(g, h):
            cv = W_VEC_COLS
            nc.scalar.copy(out=wgrp[(g, h)][:, cv:H, :].rearrange("p (c i) j -> p c j i", i=4),
                           in_=wraw[(g, h)][:, :, cv:H].rearrange("p j (c i) -> p c j i", i=4))

        def w_quant(g, h):
            nc.vector.quantize_mx(
                out=wcodes[:, g, h * H:(h + 1) * H].bitcast(FP8X4),
                scales=wscales[:, g, h * H:(h + 1) * H],
                in_=wgrp[(g, h)][:].rearrange("p n j -> p (n j)"),
            )

        xt, xg, xc, xsc, acc, v, n, fr, s, o, st = {}, {}, {}, {}, {}, {}, {}, {}, {}, {}, {}

        def x_transpose(i):
            words = xs[i][:].bitcast(F32)
            xt[i] = xtp.tile([P, NG, 2, P], F32, name="xt", tag="xt")
            for g in range(NG):
                for u in range(2):
                    nc.tensor.transpose(xt[i][:, g, u, :], words[:, 256 * g + u:256 * (g + 1):2], ident[:])

        def x_copy(i):
            xg[i] = xip.tile([P, 4 * NG * P], BF16, name="xg", tag="xg", align_bytes=64)
            nc.scalar.copy(
                out=xg[i][:].bitcast(F32).rearrange("p (g r u) -> p g r u", g=NG, u=2),
                in_=xt[i][:].rearrange("p g u r -> p g r u"),
            )

        def x_quant(i):
            xc[i] = xgp.tile([P, NG * P], U32, name="xc", tag="xc", align_bytes=64)
            xsc[i] = xgp.tile([P, NG * P], U8, name="xsc", tag="xsc", align_bytes=64)
            nc.vector.quantize_mx(out=xc[i][:].bitcast(FP8X4), scales=xsc[i][:], in_=xg[i][:])

        def mm(i, halves=(0, 1)):
            for h in halves:
                acc[(i, h)] = accp.tile([P, H], F32, name="acc", tag="acc")
                for g in range(NG):
                    nc.tensor.matmul_mx(
                        out=acc[(i, h)][:],
                        lhsT=xc[i][:, g * P:(g + 1) * P].bitcast(FP8X4),
                        lhsT_scale=xsc[i][:, g * P:(g + 1) * P],
                        rhs=wcodes[:, g, h * H:(h + 1) * H].bitcast(FP8X4),
                        rhs_scale=wscales[:, g, h * H:(h + 1) * H],
                        start=(g == 0),
                        stop=(g == NG - 1),
                    )

        def turns(i, h):
            if h == 0:
                v[i] = ep.tile([P, N], F32, name="v", tag="v")
                n[i] = ep.tile([P, N], I32, name="n", tag="n")
            cols = slice(h * H, (h + 1) * H)
            nc.vector.tensor_tensor(out=v[i][:, cols], in0=acc[(i, h)][:], in1=pb[:, cols], op=ALU.add)
            if i > 0:
                nc.gpsimd.tensor_scalar(out=n[i][:, cols], in0=v[i][:, cols], scalar1=INV2PI, scalar2=phs[:, 0:1],
                                        op0=ALU.mult, op1=ALU.add)
            elif h == 1:
                nc.vector.tensor_scalar(out=n[i][:], in0=v[i][:], scalar1=INV2PI, scalar2=phs[:, 0:1], op0=ALU.mult,
                                        op1=ALU.add)

        def frac(i):
            fr[i] = ep.tile([P, N], F32, name="fr", tag="fr")
            nc.vector.scalar_tensor_tensor(out=fr[i][:], in0=n[i][:], scalar=-TWOPI, in1=v[i][:], op0=ALU.mult,
                                           op1=ALU.add)

        def sine(i):
            s[i] = ep.tile([P, N], F32, name="s", tag="s")
            nc.scalar.activation(out=s[i][:], in_=fr[i][:], func=ACT.Sin, bias=phi, scale=1.0)

        def periodic(i):
            nc.scalar.activation(out=o[i][:, N:2 * N], in_=s[i][:], func=ACT.Identity, scale=amp[:, 0:1])
            nc.sync.dma_start(out=out_0[i * P:(i + 1) * P, N:2 * N], in_=o[i][:, N:2 * N])

        def periodic_part(i, lo, hi, pool):
            if pool:
                nc.gpsimd.tensor_scalar(out=o[i][:, N + lo:N + hi], in0=s[i][:, lo:hi], scalar1=amp[:, 0:1], scalar2=0.0,
                                        op0=ALU.mult, op1=ALU.add)
            else:
                nc.scalar.activation(out=o[i][:, N + lo:N + hi], in_=s[i][:, lo:hi], func=ACT.Identity,
                                     scale=amp[:, 0:1])

        def store_periodic(i):
            nc.sync.dma_start(out=out_0[i * P:(i + 1) * P, N:2 * N], in_=o[i][:, N:2 * N])

        def linear(i):
            o[i] = o_all[:, i * 2 * N:(i + 1) * 2 * N]
            if i == 0:
                nc.scalar.activation(out=o[i][:, 0:N], in_=xs[i][:], func=ACT.Identity, bias=p_t, scale=w_t)
            for h in range(2 if i > 0 else 0):
                cols = slice(h * H, (h + 1) * H)
                nc.gpsimd.tensor_scalar(out=o[i][:, cols], in0=xs[i][:, cols], scalar1=w_t, scalar2=p_t,
                                        op0=ALU.mult, op1=ALU.add)
            nc.sync.dma_start(out=out_0[i * P:(i + 1) * P, 0:N], in_=o[i][:, 0:N])

        def amax_linear(i):
            st[i] = op.tile([P, 24], F32, name="st", tag="st")
            nc.vector.tensor_reduce(out=st[i][:, 0:1], in_=o[i][:, 0:N], axis=AX.X, op=ALU.max,
                                    apply_absolute_value=True)

        def amax_periodic(i):
            nc.vector.tensor_reduce(out=st[i][:, 1:2], in_=o[i][:, N:2 * N], axis=AX.X, op=ALU.max,
                                    apply_absolute_value=True)

        def q_scale(i):
            nc.vector.tensor_scalar(out=st[i][:, 8:9], in0=st[i][:, 1:2], scalar1=st[i][:, 0:1], scalar2=1.0 / 448.0,
                                    op0=ALU.max, op1=ALU.mult)

        def r_scale(i):
            nc.vector.reciprocal(out=st[i][:, 16:17], in_=st[i][:, 8:9])

        o8 = {}

        def cast_tile(i):
            o8[i] = o8p.tile([P, 2 * N], FP8, name="o8", tag="o8")

        def cast_vec(i, lo, hi):
            nc.vector.tensor_scalar(out=o8[i][:, lo:hi], in0=o[i][:, lo:hi], scalar1=st[i][:, 16:17], scalar2=None,
                                    op0=ALU.mult, saturate=False)

        def cast_act(i, hi):
            nc.scalar.activation(out=o8[i][:, 0:hi], in_=o[i][:, 0:hi], func=ACT.Identity, bias=zero[:, 0:1],
                                 scale=st[i][:, 16:17], saturate=False)

        def store_bytes(i):
            nc.sync.dma_start(out=out_1[i * P:(i + 1) * P, :], in_=o8[i][:].bitcast(U8))

        w_copy_vec(0, 0)
        w_copy_act(0, 0)
        unit_vector()
        w_copy_vec(1, 0)
        w_copy_act(1, 0)
        start_slope()
        w_quant(0, 0)
        w_copy_vec(0, 1)
        x_transpose(0)
        warm_bank = accp.tile([P, H], F32, name="warm_bank", tag="acc")
        for rep_i in range(4):
            nc.tensor.matmul(warm_bank[:], lhsT=ones[:], rhs=zp[:, 0:H], start=True, stop=True)
        x_copy(0)
        start_angle()
        w_copy_act(0, 1)
        refine_terms(0)
        w_quant(1, 0)
        w_copy_vec(1, 1)
        w_copy_act(1, 1)
        refine_sum(0)
        x_quant(0)
        x_transpose(1)
        mm(0, (0,))
        nc.scalar.copy(out=pb[:], in_=pbank[:])
        refine_terms(1)
        act(u1[:], c0, ACT.Identity, scale=sw)
        refine_sum(1)
        act(amp[:], s0, ACT.Identity, scale=cw, bias=u1[:, 0:1])
        act(phs[:], phi, ACT.Copy, scale=INV2PI)
        w_quant(0, 1)
        w_quant(1, 1)
        mm(0, (1,))
        x_transpose(2)
        turns(0, 0)
        turns(0, 1)
        x_copy(1)
        x_quant(1)
        x_transpose(3)
        x_copy(2)
        x_quant(2)
        mm(1)
        x_transpose(4)
        x_copy(3)
        x_transpose(5)

        for k in range(NT):
            if k >= 1:
                turns(k, 0)
                turns(k, 1)
                sine(k - 1)
            if k in (1, 2):
                for i in (2 * k + 2, 2 * k + 3):
                    x_copy(i)
                    if i + 2 < NT:
                        x_transpose(i + 2)
            if k >= 3:
                cast_tile(k - 3)
                cast_act(k - 3, 2 * N)
                store_bytes(k - 3)
            if k >= 2:
                amax_periodic(k - 2)
            if k >= 1:
                periodic(k - 1)
                amax_linear(k - 1)
            linear(k)
            if k >= 2:
                q_scale(k - 2)
            if 3 <= k + 2 < NT:
                x_quant(k + 2)
            if k + 2 < NT:
                mm(k + 2)
            frac(k)
            if k >= 2:
                r_scale(k - 2)

        a, b, c = NT - 3, NT - 2, NT - 1
        sine(c)
        amax_periodic(b)
        periodic_part(c, 0, H, True)
        periodic_part(c, H, N, False)
        store_periodic(c)
        amax_linear(c)
        q_scale(b)
        cast_tile(a)
        cast_act(a, 2 * N)
        store_bytes(a)
        amax_periodic(c)
        r_scale(b)
        q_scale(c)
        cast_tile(b)
        cast_vec(b, TAIL_SPLIT, TAIL_SPLIT + TAIL_PIECE)
        r_scale(c)
        cast_vec(b, TAIL_SPLIT + TAIL_PIECE, 2 * N)
        cast_act(b, TAIL_SPLIT)
        store_bytes(b)
        cast_tile(c)
        cast_vec(c, 0, 2 * N)
        store_bytes(c)
